import numpy as np
import ml_dtypes


def mxq(x, axis, fmt="e4m3"):
    dtype, down = {"e4m3": (ml_dtypes.float8_e4m3fn, 7), "e5m2": (ml_dtypes.float8_e5m2, 14)}[fmt]
    v = np.moveaxis(np.asarray(x, np.float32).astype(ml_dtypes.bfloat16).astype(np.float64), axis, -1)
    blocks = v.reshape(v.shape[:-1] + (-1, 32))
    amax = np.abs(blocks).max(-1, keepdims=True)
    byte = np.maximum(np.where(amax > 0, np.frexp(amax)[1] - 1 + 127, 0) - down, 1)
    scale = np.exp2(byte - 127.0)
    codes = (blocks / scale).astype(np.float32).astype(dtype).astype(np.float64)
    return np.moveaxis((codes * scale).reshape(v.shape), -1, axis)


WIDE = False


def mx_kscale(k):
    if not WIDE:
        return np.ones(k)
    levels = np.array([10, -10, 5, -5, 0])
    a = np.random.permutation(np.resize(levels, k // 512 * 4)).reshape(k // 512, 4)
    idx = np.arange(k)
    return np.exp2(a[idx // 512, idx % 128 // 32])


BF16 = ml_dtypes.bfloat16


def bf(x):
    return np.asarray(x, np.float32).astype(BF16)


def f64(x):
    return np.asarray(x).astype(np.float64)


E2M1 = np.array([0.0, 0.5, 1.0, 1.5, 2.0, 3.0, 4.0, 6.0, -0.0, -0.5, -1.0, -1.5, -2.0, -3.0, -4.0, -6.0])


def pack_weight(w, fmt):
    k, n = w.shape
    w = f64(bf(w)).reshape(k // 32, 32, n)
    amax = np.abs(w).max(1)
    if fmt == "e4m3":
        byte = np.frexp(amax)[1] - 1 + 127 - 7
    else:
        mant, ex = np.frexp(amax / 6.0)
        byte = np.where(mant > 0.5, ex, ex - 1) + 127
    byte = np.clip(np.where(amax > 0, byte, 1), 1, 254)
    scaled = (w * np.exp2(127.0 - byte)[:, None, :]).reshape(k, n).astype(np.float32)
    by_word = np.ascontiguousarray(scaled.reshape(k // 512, 128, 4, n).transpose(0, 1, 3, 2))
    if fmt == "e4m3":
        words = by_word.astype(ml_dtypes.float8_e4m3fn).view(np.uint8)
    else:
        c = by_word.astype(ml_dtypes.float4_e2m1fn).view(np.uint8) & 0xF
        words = c[..., 0::2] | (c[..., 1::2] << 4)
    return np.ascontiguousarray(words), np.ascontiguousarray(byte.astype(np.uint8).reshape(k // 512, 16, n))


def unpack_weight(words, scales, fmt):
    g, p, n, _ = words.shape
    if fmt == "e4m3":
        vals = np.ascontiguousarray(words).view(ml_dtypes.float8_e4m3fn).astype(np.float64)
    else:
        nib = np.empty((g, p, n, 4), np.uint8)
        nib[..., 0::2] = words & 0xF
        nib[..., 1::2] = words >> 4
        vals = E2M1[nib]
    vals = vals * np.repeat(np.exp2(scales.astype(np.float64) - 127.0), 8, axis=1)[..., None]
    return vals.transpose(0, 1, 3, 2).reshape(g * 512, n)


B, IN, OUT = 128, 8192, 4096
QI, QO = IN // 4, OUT // 4
FMT = "e4m3"


def _hamilton_weight(Wr, Wi, Wj, Wk):
    return np.concatenate([
        np.concatenate([Wr, Wi, Wj, Wk], axis=1),
        np.concatenate([-Wi, Wr, Wk, -Wj], axis=1),
        np.concatenate([-Wj, -Wk, Wr, Wi], axis=1),
        np.concatenate([-Wk, Wj, -Wi, Wr], axis=1),
    ], axis=0)


def _hamilton_bias(br, bi, bj, bk):
    return np.concatenate([
        br - bi - bj - bk,
        br + bi + bj - bk,
        br - bi + bj + bk,
        br + bi - bj + bk,
    ], axis=0)


def setup_inputs():
    s = mx_kscale(IN)[:QI]
    c = 1.0 / np.sqrt(QI)
    x = bf(np.random.standard_normal((B, IN)) * np.tile(s, 4))
    Wr_words, Wr_scales = pack_weight(np.random.standard_normal((QI, QO)) * c / s[:, None], FMT)
    Wi_words, Wi_scales = pack_weight(np.random.standard_normal((QI, QO)) * c / s[:, None], FMT)
    Wj_words, Wj_scales = pack_weight(np.random.standard_normal((QI, QO)) * c / s[:, None], FMT)
    Wk_words, Wk_scales = pack_weight(np.random.standard_normal((QI, QO)) * c / s[:, None], FMT)
    return {"x": x,
            "Wr_words": Wr_words, "Wr_scales": Wr_scales,
            "Wi_words": Wi_words, "Wi_scales": Wi_scales,
            "Wj_words": Wj_words, "Wj_scales": Wj_scales,
            "Wk_words": Wk_words, "Wk_scales": Wk_scales,
            "br": bf(np.random.standard_normal(QO) * 0.3),
            "bi": bf(np.random.standard_normal(QO) * 0.3),
            "bj": bf(np.random.standard_normal(QO) * 0.3),
            "bk": bf(np.random.standard_normal(QO) * 0.3)}


def reference(x, Wr_words, Wr_scales, Wi_words, Wi_scales, Wj_words, Wj_scales, Wk_words, Wk_scales, br, bi, bj, bk):
    W = _hamilton_weight(unpack_weight(Wr_words, Wr_scales, FMT),
                         unpack_weight(Wi_words, Wi_scales, FMT),
                         unpack_weight(Wj_words, Wj_scales, FMT),
                         unpack_weight(Wk_words, Wk_scales, FMT))
    b = _hamilton_bias(f64(br), f64(bi), f64(bj), f64(bk))
    return (mxq(f64(x), 1, "e4m3") @ W) + b

@@ -1,0 +1,194 @@
+from contextlib import ExitStack
+
+import concourse.mybir as mybir
+from concourse.masks import make_identity
+
+F32 = mybir.dt.float32
+BF16 = mybir.dt.bfloat16
+I32 = mybir.dt.int32
+U32 = mybir.dt.uint32
+U8 = mybir.dt.uint8
+FP8X4 = mybir.dt.float8_e4m3fn_x4
+
+P = 128
+PACK = 4
+K_PASS = P * PACK
+C = 4
+QI = 2048
+QO = 1024
+G = QI // K_PASS
+N_TILE = 512
+H = QO // N_TILE
+PLUS, MINUS = 0, 1
+
+FLOPS = 2 * P * (C * QI) * (C * QO)
+
+HAMILTON = (
+    ((0, PLUS), (1, PLUS), (2, PLUS), (3, PLUS)),
+    ((1, MINUS), (0, PLUS), (3, PLUS), (2, MINUS)),
+    ((2, MINUS), (3, MINUS), (0, PLUS), (1, PLUS)),
+    ((3, MINUS), (2, PLUS), (1, MINUS), (0, PLUS)),
+)
+BIAS_SIGN = (
+    (1.0, -1.0, -1.0, -1.0),
+    (1.0, 1.0, 1.0, -1.0),
+    (1.0, -1.0, 1.0, 1.0),
+    (1.0, 1.0, -1.0, 1.0),
+)
+
+
+def tile_quaternionlinear_w_kernel(
+    tc, x,
+    Wr_words, Wr_scales, Wi_words, Wi_scales, Wj_words, Wj_scales, Wk_words, Wk_scales,
+    br, bi, bj, bk,
+    out,
+):
+    nc = tc.nc
+    words_in = (Wr_words, Wi_words, Wj_words, Wk_words)
+    scales_in = (Wr_scales, Wi_scales, Wj_scales, Wk_scales)
+    bias_in = (br, bi, bj, bk)
+
+    with ExitStack() as ctx:
+        const = ctx.enter_context(tc.tile_pool(name="const", bufs=1))
+        x_pool = ctx.enter_context(tc.tile_pool(name="x_pool", bufs=G))
+        plane_pool = ctx.enter_context(tc.tile_pool(name="plane_pool", bufs=C))
+        weight_pool = ctx.enter_context(tc.tile_pool(name="weight_pool", bufs=C * G * H))
+        bias_pool = ctx.enter_context(tc.tile_pool(name="bias_pool", bufs=C * H))
+        stage = ctx.enter_context(tc.tile_pool(name="stage", bufs=4))
+        psum = ctx.enter_context(tc.psum_pool(name="psum", bufs=8))
+        ctx.enter_context(tc.manual_schedule())
+
+        bias_rows = const.tile([P, QO], BF16)
+        nc.vector.memset(bias_rows[:], 0.0)
+        for w in range(C):
+            nc.scalar.dma_start(
+                out=bias_rows[32 * w : 32 * w + 1, :],
+                in_=bias_in[w].rearrange("(a n) -> a n", a=1),
+            )
+        signs = const.tile([P, C, P], BF16)
+        nc.vector.memset(signs[:], 1.0)
+        for o in range(C):
+            for w in range(C):
+                if BIAS_SIGN[o][w] < 0:
+                    nc.vector.memset(signs[32 * w : 32 * w + 32, o, :], -1.0)
+        identity = const.tile([P, P], F32)
+        make_identity(nc, identity[:])
+
+        x_by_group = x.rearrange("m (c g k) -> m g c k", c=C, g=G)
+        x_rows_of = []
+        for g in range(G):
+            x_rows = x_pool.tile([P, C, K_PASS], BF16)
+            nc.sync.dma_start(out=x_rows[:], in_=x_by_group[:, g])
+            x_rows_of.append(x_rows)
+
+        planes_of = []
+        for w in range(C):
+            planes = plane_pool.tile([P, QO], U8, align_bytes=64)
+            nc.vector.memset(planes[:].bitcast(I32), 0)
+            planes_of.append(planes)
+
+        w_codes_of = {}
+        for h in range(H):
+            for g in range(G):
+                for w in range(C):
+                    if h == 0 and g == 0:
+                        for quadrant in range(4):
+                            nc.sync.dma_start(
+                                out=planes_of[w][32 * quadrant : 32 * quadrant + 16, :].bitcast(I32),
+                                in_=scales_in[w][:, 4 * quadrant : 4 * quadrant + 4, :].bitcast(I32),
+                            )
+                    w_codes = weight_pool.tile([P, N_TILE], U32, align_bytes=64)
+                    all_bytes = words_in[w][g].rearrange("p n t -> p (n t)")
+                    nc.sync.dma_start(
+                        out=w_codes[:].bitcast(I32),
+                        in_=all_bytes[:, PACK * N_TILE * h : PACK * N_TILE * (h + 1)].bitcast(I32),
+                    )
+                    w_codes_of[(w, g, h)] = w_codes
+
+        bias_of = {}
+        x_codes_of = []
+        x_scales_of = []
+        for g in range(G):
+            for b in range(2):
+                o, h = divmod(2 * g + b, H)
+                bias_bank = psum.tile([P, N_TILE], F32, tag="bank")
+                nc.tensor.matmul(
+                    out=bias_bank[:],
+                    lhsT=signs[:, o, :],
+                    rhs=bias_rows[:, N_TILE * h : N_TILE * (h + 1)],
+                    start=True,
+                    stop=True,
+                )
+                bias = bias_pool.tile([P, N_TILE], F32)
+                if b == 0:
+                    nc.vector.tensor_copy(out=bias[:], in_=bias_bank[:])
+                else:
+                    nc.scalar.copy(out=bias[:], in_=bias_bank[:])
+                bias_of[(o, h)] = bias
+
+            grouped = x_pool.tile([P, 2, C, P, PACK], BF16, align_bytes=64)
+            for pair in range(C // 2):
+                flipped = psum.tile([P, 2, 2, P], F32, tag="bank")
+                for j in range(2):
+                    x_words = x_rows_of[g][:, 2 * pair + j, :].bitcast(F32)
+                    for u in range(2):
+                        nc.tensor.transpose(
+                            flipped[:, j, u, :], x_words[:, u : K_PASS // 2 : 2], identity[:]
+                        )
+                nc.scalar.copy(
+                    out=grouped[:, PLUS, 2 * pair : 2 * pair + 2, :, :].bitcast(F32),
+                    in_=flipped[:].rearrange("p j u m -> p j m u"),
+                )
+            nc.vector.tensor_scalar_mul(
+                out=grouped[:, MINUS].rearrange("p c m t -> p (c m t)"),
+                in0=grouped[:, PLUS].rearrange("p c m t -> p (c m t)"),
+                scalar1=-1.0,
+            )
+            x_codes = x_pool.tile([P, 2, C, P], U32, align_bytes=64)
+            x_scales = x_pool.tile([P, 2, C, P], U8, align_bytes=64)
+            nc.vector.quantize_mx(
+                out=x_codes[:].rearrange("p s c m -> p (s c m)").bitcast(FP8X4),
+                scales=x_scales[:].rearrange("p s c m -> p (s c m)"),
+                in_=grouped[:].rearrange("p s c m t -> p (s c m t)"),
+            )
+            x_codes_of.append(x_codes)
+            x_scales_of.append(x_scales)
+
+        def one_pass(acc, o, h, g, w):
+            c = [HAMILTON[row][o][0] for row in range(C)].index(w)
+            copy_of_x = HAMILTON[c][o][1]
+            nc.tensor.matmul_mx(
+                out=acc[:],
+                lhsT=x_codes_of[g][:, copy_of_x, c, :].bitcast(FP8X4),
+                lhsT_scale=x_scales_of[g][:, copy_of_x, c, :],
+                rhs=w_codes_of[(w, g, h)][:].bitcast(FP8X4),
+                rhs_scale=planes_of[w][PACK * g : P, N_TILE * h : N_TILE * (h + 1)],
+                start=(g == 0 and w == 0),
+                stop=(g == G - 1 and w == C - 1),
+            )
+
+        def finish(acc, o, h):
+            result = stage.tile([P, N_TILE], F32)
+            nc.vector.tensor_tensor(
+                out=result[:], in0=acc[:], in1=bias_of[(o, h)][:], op=mybir.AluOpType.add
+            )
+            first = QO * o + N_TILE * h
+            nc.sync.dma_start(out=out[:, first : first + N_TILE], in_=result[:])
+
+        acc_of = []
+        for o in range(C):
+            acc = psum.tile([P, N_TILE], F32, tag="bank")
+            acc_of.append(acc)
+        for g in range(G):
+            for w in range(C):
+                for o in range(C):
+                    one_pass(acc_of[o], o, 0, g, w)
+        for o in range(C):
+            finish(acc_of[o], o, 0)
+
+        for o in range(C):
+            acc = psum.tile([P, N_TILE], F32, tag="bank")
+            for g in range(G):
+                for w in range(C):
+                    one_pass(acc, o, 1, g, w)
+            finish(acc, o, 1)

@@ -29,12 +29,8 @@ HAMILTON = (
     ((2, MINUS), (3, MINUS), (0, PLUS), (1, PLUS)),
     ((3, MINUS), (2, PLUS), (1, MINUS), (0, PLUS)),
 )
-BIAS_SIGN = (
-    (1.0, -1.0, -1.0, -1.0),
-    (1.0, 1.0, 1.0, -1.0),
-    (1.0, -1.0, 1.0, 1.0),
-    (1.0, 1.0, -1.0, 1.0),
-)
+SQUARE = 32
+TAIL_PIECES = 2
 
 
 def tile_quaternionlinear_w_kernel(
@@ -47,39 +43,30 @@ def tile_quaternionlinear_w_kernel(
     words_in = (Wr_words, Wi_words, Wj_words, Wk_words)
     scales_in = (Wr_scales, Wi_scales, Wj_scales, Wk_scales)
     bias_in = (br, bi, bj, bk)
+    add = mybir.AluOpType.add
+    subtract = mybir.AluOpType.subtract
 
     with ExitStack() as ctx:
         const = ctx.enter_context(tc.tile_pool(name="const", bufs=1))
+        x_in_pool = ctx.enter_context(tc.tile_pool(name="x_in_pool", bufs=2 * G))
         x_pool = ctx.enter_context(tc.tile_pool(name="x_pool", bufs=G))
         plane_pool = ctx.enter_context(tc.tile_pool(name="plane_pool", bufs=C))
         weight_pool = ctx.enter_context(tc.tile_pool(name="weight_pool", bufs=C * G * H))
-        bias_pool = ctx.enter_context(tc.tile_pool(name="bias_pool", bufs=C * H))
+        bias_pool = ctx.enter_context(tc.tile_pool(name="bias_pool", bufs=2))
         stage = ctx.enter_context(tc.tile_pool(name="stage", bufs=4))
         psum = ctx.enter_context(tc.psum_pool(name="psum", bufs=8))
         ctx.enter_context(tc.manual_schedule())
 
-        bias_rows = const.tile([P, QO], BF16)
-        nc.vector.memset(bias_rows[:], 0.0)
-        for w in range(C):
-            nc.scalar.dma_start(
-                out=bias_rows[32 * w : 32 * w + 1, :],
-                in_=bias_in[w].rearrange("(a n) -> a n", a=1),
-            )
-        signs = const.tile([P, C, P], BF16)
-        nc.vector.memset(signs[:], 1.0)
-        for o in range(C):
-            for w in range(C):
-                if BIAS_SIGN[o][w] < 0:
-                    nc.vector.memset(signs[32 * w : 32 * w + 32, o, :], -1.0)
         identity = const.tile([P, P], F32)
         make_identity(nc, identity[:])
 
         x_by_group = x.rearrange("m (c g k) -> m g c k", c=C, g=G)
-        x_rows_of = []
+        x_rows_of = {}
         for g in range(G):
-            x_rows = x_pool.tile([P, C, K_PASS], BF16)
-            nc.sync.dma_start(out=x_rows[:], in_=x_by_group[:, g])
-            x_rows_of.append(x_rows)
+            for pair in range(C // 2):
+                x_rows = x_in_pool.tile([P, 2, K_PASS], BF16)
+                nc.sync.dma_start(out=x_rows[:], in_=x_by_group[:, g, 2 * pair : 2 * pair + 2, :])
+                x_rows_of[(g, pair)] = x_rows
 
         planes_of = []
         for w in range(C):
@@ -89,14 +76,14 @@ def tile_quaternionlinear_w_kernel(
 
         w_codes_of = {}
         for h in range(H):
-            for g in range(G):
-                for w in range(C):
-                    if h == 0 and g == 0:
-                        for quadrant in range(4):
-                            nc.sync.dma_start(
-                                out=planes_of[w][32 * quadrant : 32 * quadrant + 16, :].bitcast(I32),
-                                in_=scales_in[w][:, 4 * quadrant : 4 * quadrant + 4, :].bitcast(I32),
-                            )
+            for w in range(C):
+                if h == 0:
+                    for quadrant in range(4):
+                        nc.sync.dma_start(
+                            out=planes_of[w][32 * quadrant : 32 * quadrant + 16, :].bitcast(I32),
+                            in_=scales_in[w][:, 4 * quadrant : 4 * quadrant + 4, :].bitcast(I32),
+                        )
+                for g in range(G):
                     w_codes = weight_pool.tile([P, N_TILE], U32, align_bytes=64)
                     all_bytes = words_in[w][g].rearrange("p n t -> p (n t)")
                     nc.sync.dma_start(
@@ -105,90 +92,129 @@ def tile_quaternionlinear_w_kernel(
                     )
                     w_codes_of[(w, g, h)] = w_codes
 
-        bias_of = {}
+        folded = const.tile([P, C, SQUARE], BF16)
+        for w in range(C):
+            nc.gpsimd.dma_start(
+                out=folded[:, w, :],
+                in_=bias_in[w]
+                .rearrange("(a i) -> a i", i=SQUARE)
+                .unsqueeze(0)
+                .to_broadcast([P // SQUARE, SQUARE, SQUARE]),
+            )
+
+        grouped_of = {}
         x_codes_of = []
         x_scales_of = []
-        for g in range(G):
-            for b in range(2):
-                o, h = divmod(2 * g + b, H)
-                bias_bank = psum.tile([P, N_TILE], F32, tag="bank")
-                nc.tensor.matmul(
-                    out=bias_bank[:],
-                    lhsT=signs[:, o, :],
-                    rhs=bias_rows[:, N_TILE * h : N_TILE * (h + 1)],
-                    start=True,
-                    stop=True,
-                )
-                bias = bias_pool.tile([P, N_TILE], F32)
-                if b == 0:
-                    nc.vector.tensor_copy(out=bias[:], in_=bias_bank[:])
-                else:
-                    nc.scalar.copy(out=bias[:], in_=bias_bank[:])
-                bias_of[(o, h)] = bias
 
-            grouped = x_pool.tile([P, 2, C, P, PACK], BF16, align_bytes=64)
+        def quantise(g, copy_of_x):
+            nc.vector.quantize_mx(
+                out=x_codes_of[g][:, copy_of_x].rearrange("p c m -> p (c m)").bitcast(FP8X4),
+                scales=x_scales_of[g][:, copy_of_x].rearrange("p c m -> p (c m)"),
+                in_=grouped_of[(g, copy_of_x)][:].rearrange("p c m t -> p (c m t)"),
+            )
+
+        def negate_and_quantise(g):
+            minus = x_pool.tile([P, C, P, PACK], BF16, align_bytes=64)
+            nc.vector.tensor_scalar_mul(
+                out=minus[:].rearrange("p c m t -> p (c m t)"),
+                in0=grouped_of[(g, PLUS)][:].rearrange("p c m t -> p (c m t)"),
+                scalar1=-1.0,
+            )
+            grouped_of[(g, MINUS)] = minus
+            quantise(g, MINUS)
+
+        for g in range(G):
+            plus = x_pool.tile([P, C, P, PACK], BF16, align_bytes=64)
             for pair in range(C // 2):
                 flipped = psum.tile([P, 2, 2, P], F32, tag="bank")
                 for j in range(2):
-                    x_words = x_rows_of[g][:, 2 * pair + j, :].bitcast(F32)
+                    x_words = x_rows_of[(g, pair)][:, j, :].bitcast(F32)
                     for u in range(2):
                         nc.tensor.transpose(
                             flipped[:, j, u, :], x_words[:, u : K_PASS // 2 : 2], identity[:]
                         )
                 nc.scalar.copy(
-                    out=grouped[:, PLUS, 2 * pair : 2 * pair + 2, :, :].bitcast(F32),
+                    out=plus[:, 2 * pair : 2 * pair + 2, :, :].bitcast(F32),
                     in_=flipped[:].rearrange("p j u m -> p j m u"),
                 )
-            nc.vector.tensor_scalar_mul(
-                out=grouped[:, MINUS].rearrange("p c m t -> p (c m t)"),
-                in0=grouped[:, PLUS].rearrange("p c m t -> p (c m t)"),
-                scalar1=-1.0,
-            )
+            grouped_of[(g, PLUS)] = plus
             x_codes = x_pool.tile([P, 2, C, P], U32, align_bytes=64)
             x_scales = x_pool.tile([P, 2, C, P], U8, align_bytes=64)
-            nc.vector.quantize_mx(
-                out=x_codes[:].rearrange("p s c m -> p (s c m)").bitcast(FP8X4),
-                scales=x_scales[:].rearrange("p s c m -> p (s c m)"),
-                in_=grouped[:].rearrange("p s c m t -> p (s c m t)"),
-            )
             x_codes_of.append(x_codes)
             x_scales_of.append(x_scales)
+            quantise(g, PLUS)
+            if g > 0:
+                negate_and_quantise(g - 1)
+        negate_and_quantise(G - 1)
 
-        def one_pass(acc, o, h, g, w):
+        r_minus_k = const.tile([P, SQUARE], F32)
+        r_plus_k = const.tile([P, SQUARE], F32)
+        i_plus_j = const.tile([P, SQUARE], F32)
+        i_minus_j = const.tile([P, SQUARE], F32)
+        nc.vector.tensor_tensor(out=r_minus_k[:], in0=folded[:, 0, :], in1=folded[:, 3, :], op=subtract)
+        nc.vector.tensor_tensor(out=r_plus_k[:], in0=folded[:, 0, :], in1=folded[:, 3, :], op=add)
+        nc.vector.tensor_tensor(out=i_plus_j[:], in0=folded[:, 1, :], in1=folded[:, 2, :], op=add)
+        nc.vector.tensor_tensor(out=i_minus_j[:], in0=folded[:, 1, :], in1=folded[:, 2, :], op=subtract)
+        combined = const.tile([P, C, SQUARE], F32, align_bytes=64)
+        nc.vector.tensor_tensor(out=combined[:, 0, :], in0=r_minus_k[:], in1=i_plus_j[:], op=subtract)
+        nc.vector.tensor_tensor(out=combined[:, 1, :], in0=r_minus_k[:], in1=i_plus_j[:], op=add)
+        nc.vector.tensor_tensor(out=combined[:, 2, :], in0=r_plus_k[:], in1=i_minus_j[:], op=subtract)
+        nc.vector.tensor_tensor(out=combined[:, 3, :], in0=r_plus_k[:], in1=i_minus_j[:], op=add)
+        upright = const.tile([P, C * SQUARE], F32, align_bytes=64)
+        nc.vector.transpose(out=upright[:], in_=combined[:].rearrange("p o i -> p (o i)"))
+        bias_of = []
+        for s in range(2):
+            repeated = bias_pool.tile([P, 2 * SQUARE, SQUARE], F32, align_bytes=64)
+            nc.scalar.copy(
+                out=repeated[:],
+                in_=upright[:, 2 * SQUARE * s : 2 * SQUARE * (s + 1)]
+                .unsqueeze(2)
+                .to_broadcast([P, 2 * SQUARE, SQUARE]),
+            )
+            bias = bias_pool.tile([P, 2 * QO], F32, align_bytes=64)
+            nc.vector.transpose(out=bias[:], in_=repeated[:].rearrange("p b j -> p (b j)"))
+            bias_of.append(bias)
+
+        def one_pass(acc, o, first, width, w, g):
             c = [HAMILTON[row][o][0] for row in range(C)].index(w)
             copy_of_x = HAMILTON[c][o][1]
+            h, inside = divmod(first, N_TILE)
             nc.tensor.matmul_mx(
                 out=acc[:],
                 lhsT=x_codes_of[g][:, copy_of_x, c, :].bitcast(FP8X4),
                 lhsT_scale=x_scales_of[g][:, copy_of_x, c, :],
-                rhs=w_codes_of[(w, g, h)][:].bitcast(FP8X4),
-                rhs_scale=planes_of[w][PACK * g : P, N_TILE * h : N_TILE * (h + 1)],
-                start=(g == 0 and w == 0),
-                stop=(g == G - 1 and w == C - 1),
+                rhs=w_codes_of[(w, g, h)][:, inside : inside + width].bitcast(FP8X4),
+                rhs_scale=planes_of[w][PACK * g : P, first : first + width],
+                start=(w == 0 and g == 0),
+                stop=(w == C - 1 and g == G - 1),
             )
 
-        def finish(acc, o, h):
-            result = stage.tile([P, N_TILE], F32)
+        def finish(acc, o, first, width):
+            result = stage.tile([P, width], F32, tag="result")
+            in_bias = QO * (o % 2) + first
             nc.vector.tensor_tensor(
-                out=result[:], in0=acc[:], in1=bias_of[(o, h)][:], op=mybir.AluOpType.add
+                out=result[:], in0=acc[:], in1=bias_of[o // 2][:, in_bias : in_bias + width], op=add
             )
-            first = QO * o + N_TILE * h
-            nc.sync.dma_start(out=out[:, first : first + N_TILE], in_=result[:])
+            nc.sync.dma_start(out=out[:, QO * o + first : QO * o + first + width], in_=result[:])
 
         acc_of = []
         for o in range(C):
             acc = psum.tile([P, N_TILE], F32, tag="bank")
             acc_of.append(acc)
-        for g in range(G):
-            for w in range(C):
+        for w in range(C):
+            for g in range(G):
                 for o in range(C):
-                    one_pass(acc_of[o], o, 0, g, w)
+                    one_pass(acc_of[o], o, 0, N_TILE, w, g)
         for o in range(C):
-            finish(acc_of[o], o, 0)
+            finish(acc_of[o], o, 0, N_TILE)
 
         for o in range(C):
-            acc = psum.tile([P, N_TILE], F32, tag="bank")
-            for g in range(G):
+            pieces = TAIL_PIECES if o == C - 1 else 1
+            width = N_TILE // pieces
+            for piece in range(pieces):
+                first = N_TILE + width * piece
+                acc = psum.tile([P, width], F32, tag="bank")
                 for w in range(C):
-                    one_pass(acc, o, 1, g, w)
-            finish(acc, o, 1)
+                    for g in range(G):
+                        one_pass(acc, o, first, width, w, g)
+                finish(acc, o, first, width)

@@ -30,7 +30,6 @@ HAMILTON = (
     ((3, MINUS), (2, PLUS), (1, MINUS), (0, PLUS)),
 )
 SQUARE = 32
-TAIL_PIECES = 2
 
 
 def tile_quaternionlinear_w_kernel(
@@ -48,10 +47,9 @@ def tile_quaternionlinear_w_kernel(
 
     with ExitStack() as ctx:
         const = ctx.enter_context(tc.tile_pool(name="const", bufs=1))
-        x_in_pool = ctx.enter_context(tc.tile_pool(name="x_in_pool", bufs=2 * G))
-        x_pool = ctx.enter_context(tc.tile_pool(name="x_pool", bufs=G))
+        x_pool = ctx.enter_context(tc.tile_pool(name="x_pool", bufs=C))
         plane_pool = ctx.enter_context(tc.tile_pool(name="plane_pool", bufs=C))
-        weight_pool = ctx.enter_context(tc.tile_pool(name="weight_pool", bufs=C * G * H))
+        weight_pool = ctx.enter_context(tc.tile_pool(name="weight_pool", bufs=C * G))
         bias_pool = ctx.enter_context(tc.tile_pool(name="bias_pool", bufs=2))
         stage = ctx.enter_context(tc.tile_pool(name="stage", bufs=4))
         psum = ctx.enter_context(tc.psum_pool(name="psum", bufs=8))
@@ -60,13 +58,11 @@ def tile_quaternionlinear_w_kernel(
         identity = const.tile([P, P], F32)
         make_identity(nc, identity[:])
 
-        x_by_group = x.rearrange("m (c g k) -> m g c k", c=C, g=G)
-        x_rows_of = {}
-        for g in range(G):
-            for pair in range(C // 2):
-                x_rows = x_in_pool.tile([P, 2, K_PASS], BF16)
-                nc.sync.dma_start(out=x_rows[:], in_=x_by_group[:, g, 2 * pair : 2 * pair + 2, :])
-                x_rows_of[(g, pair)] = x_rows
+        x_rows_of = []
+        for c in range(C):
+            x_rows = x_pool.tile([P, QI], BF16)
+            nc.sync.dma_start(out=x_rows[:], in_=x[:, QI * c : QI * (c + 1)])
+            x_rows_of.append(x_rows)
 
         planes_of = []
         for w in range(C):
@@ -75,22 +71,19 @@ def tile_quaternionlinear_w_kernel(
             planes_of.append(planes)
 
         w_codes_of = {}
-        for h in range(H):
-            for w in range(C):
-                if h == 0:
-                    for quadrant in range(4):
-                        nc.sync.dma_start(
-                            out=planes_of[w][32 * quadrant : 32 * quadrant + 16, :].bitcast(I32),
-                            in_=scales_in[w][:, 4 * quadrant : 4 * quadrant + 4, :].bitcast(I32),
-                        )
-                for g in range(G):
-                    w_codes = weight_pool.tile([P, N_TILE], U32, align_bytes=64)
-                    all_bytes = words_in[w][g].rearrange("p n t -> p (n t)")
-                    nc.sync.dma_start(
-                        out=w_codes[:].bitcast(I32),
-                        in_=all_bytes[:, PACK * N_TILE * h : PACK * N_TILE * (h + 1)].bitcast(I32),
-                    )
-                    w_codes_of[(w, g, h)] = w_codes
+        for w in range(C):
+            for quadrant in range(4):
+                nc.sync.dma_start(
+                    out=planes_of[w][32 * quadrant : 32 * quadrant + 16, :].bitcast(I32),
+                    in_=scales_in[w][:, 4 * quadrant : 4 * quadrant + 4, :].bitcast(I32),
+                )
+            for g in range(G):
+                w_codes = weight_pool.tile([P, QO], U32, align_bytes=64)
+                nc.sync.dma_start(
+                    out=w_codes[:].bitcast(I32),
+                    in_=words_in[w][g].rearrange("p n t -> p (n t)").bitcast(I32),
+                )
+                w_codes_of[(w, g)] = w_codes
 
         folded = const.tile([P, C, SQUARE], BF16)
         for w in range(C):
@@ -106,46 +99,47 @@ def tile_quaternionlinear_w_kernel(
         x_codes_of = []
         x_scales_of = []
 
-        def quantise(g, copy_of_x):
+        def quantise(c, copy_of_x):
             nc.vector.quantize_mx(
-                out=x_codes_of[g][:, copy_of_x].rearrange("p c m -> p (c m)").bitcast(FP8X4),
-                scales=x_scales_of[g][:, copy_of_x].rearrange("p c m -> p (c m)"),
-                in_=grouped_of[(g, copy_of_x)][:].rearrange("p c m t -> p (c m t)"),
+                out=x_codes_of[c][:, copy_of_x].rearrange("p g m -> p (g m)").bitcast(FP8X4),
+                scales=x_scales_of[c][:, copy_of_x].rearrange("p g m -> p (g m)"),
+                in_=grouped_of[(c, copy_of_x)][:].rearrange("p g m t -> p (g m t)"),
             )
 
-        def negate_and_quantise(g):
-            minus = x_pool.tile([P, C, P, PACK], BF16, align_bytes=64)
-            nc.vector.tensor_scalar_mul(
-                out=minus[:].rearrange("p c m t -> p (c m t)"),
-                in0=grouped_of[(g, PLUS)][:].rearrange("p c m t -> p (c m t)"),
-                scalar1=-1.0,
-            )
-            grouped_of[(g, MINUS)] = minus
-            quantise(g, MINUS)
-
-        for g in range(G):
-            plus = x_pool.tile([P, C, P, PACK], BF16, align_bytes=64)
-            for pair in range(C // 2):
+        for c in range(C):
+            x_words = x_rows_of[c][:].bitcast(F32)
+            words_in_group = K_PASS // 2
+            plus = x_pool.tile([P, G, P, PACK], BF16, align_bytes=64)
+            for pair in range(G // 2):
                 flipped = psum.tile([P, 2, 2, P], F32, tag="bank")
                 for j in range(2):
-                    x_words = x_rows_of[(g, pair)][:, j, :].bitcast(F32)
+                    g = 2 * pair + j
                     for u in range(2):
                         nc.tensor.transpose(
-                            flipped[:, j, u, :], x_words[:, u : K_PASS // 2 : 2], identity[:]
+                            flipped[:, j, u, :],
+                            x_words[:, words_in_group * g + u : words_in_group * (g + 1) : 2],
+                            identity[:],
                         )
                 nc.scalar.copy(
                     out=plus[:, 2 * pair : 2 * pair + 2, :, :].bitcast(F32),
                     in_=flipped[:].rearrange("p j u m -> p j m u"),
                 )
-            grouped_of[(g, PLUS)] = plus
-            x_codes = x_pool.tile([P, 2, C, P], U32, align_bytes=64)
-            x_scales = x_pool.tile([P, 2, C, P], U8, align_bytes=64)
+            grouped_of[(c, PLUS)] = plus
+            x_codes = x_pool.tile([P, 2, G, P], U32, align_bytes=64)
+            x_scales = x_pool.tile([P, 2, G, P], U8, align_bytes=64)
             x_codes_of.append(x_codes)
             x_scales_of.append(x_scales)
-            quantise(g, PLUS)
-            if g > 0:
-                negate_and_quantise(g - 1)
-        negate_and_quantise(G - 1)
+            quantise(c, PLUS)
+
+        for c in range(1, C):
+            minus = x_pool.tile([P, G, P, PACK], BF16, align_bytes=64)
+            nc.vector.tensor_scalar_mul(
+                out=minus[:].rearrange("p g m t -> p (g m t)"),
+                in0=grouped_of[(c, PLUS)][:].rearrange("p g m t -> p (g m t)"),
+                scalar1=-1.0,
+            )
+            grouped_of[(c, MINUS)] = minus
+            quantise(c, MINUS)
 
         r_minus_k = const.tile([P, SQUARE], F32)
         r_plus_k = const.tile([P, SQUARE], F32)
@@ -175,46 +169,42 @@ def tile_quaternionlinear_w_kernel(
             nc.vector.transpose(out=bias[:], in_=repeated[:].rearrange("p b j -> p (b j)"))
             bias_of.append(bias)
 
-        def one_pass(acc, o, first, width, w, g):
+        acc_of = {}
+        for o in range(C):
+            for h in range(H):
+                acc = psum.tile([P, N_TILE], F32, tag="bank")
+                acc_of[(o, h)] = acc
+
+        def one_pass(o, h, w, g):
             c = [HAMILTON[row][o][0] for row in range(C)].index(w)
             copy_of_x = HAMILTON[c][o][1]
-            h, inside = divmod(first, N_TILE)
             nc.tensor.matmul_mx(
-                out=acc[:],
-                lhsT=x_codes_of[g][:, copy_of_x, c, :].bitcast(FP8X4),
-                lhsT_scale=x_scales_of[g][:, copy_of_x, c, :],
-                rhs=w_codes_of[(w, g, h)][:, inside : inside + width].bitcast(FP8X4),
-                rhs_scale=planes_of[w][PACK * g : P, first : first + width],
+                out=acc_of[(o, h)][:],
+                lhsT=x_codes_of[c][:, copy_of_x, g, :].bitcast(FP8X4),
+                lhsT_scale=x_scales_of[c][:, copy_of_x, g, :],
+                rhs=w_codes_of[(w, g)][:, N_TILE * h : N_TILE * (h + 1)].bitcast(FP8X4),
+                rhs_scale=planes_of[w][PACK * g : P, N_TILE * h : N_TILE * (h + 1)],
                 start=(w == 0 and g == 0),
                 stop=(w == C - 1 and g == G - 1),
             )
 
-        def finish(acc, o, first, width):
-            result = stage.tile([P, width], F32, tag="result")
-            in_bias = QO * (o % 2) + first
-            nc.vector.tensor_tensor(
-                out=result[:], in0=acc[:], in1=bias_of[o // 2][:, in_bias : in_bias + width], op=add
-            )
-            nc.sync.dma_start(out=out[:, QO * o + first : QO * o + first + width], in_=result[:])
-
-        acc_of = []
-        for o in range(C):
-            acc = psum.tile([P, N_TILE], F32, tag="bank")
-            acc_of.append(acc)
-        for w in range(C):
+        for w in range(C - 1):
             for g in range(G):
                 for o in range(C):
-                    one_pass(acc_of[o], o, 0, N_TILE, w, g)
-        for o in range(C):
-            finish(acc_of[o], o, 0, N_TILE)
+                    for h in range(H):
+                        one_pass(o, h, w, g)
 
         for o in range(C):
-            pieces = TAIL_PIECES if o == C - 1 else 1
-            width = N_TILE // pieces
-            for piece in range(pieces):
-                first = N_TILE + width * piece
-                acc = psum.tile([P, width], F32, tag="bank")
-                for w in range(C):
-                    for g in range(G):
-                        one_pass(acc, o, first, width, w, g)
-                finish(acc, o, first, width)
+            for h in range(H):
+                for g in range(G):
+                    one_pass(o, h, C - 1, g)
+                result = stage.tile([P, N_TILE], F32)
+                in_bias = QO * (o % 2) + N_TILE * h
+                nc.vector.tensor_tensor(
+                    out=result[:],
+                    in0=acc_of[(o, h)][:],
+                    in1=bias_of[o // 2][:, in_bias : in_bias + N_TILE],
+                    op=add,
+                )
+                first = QO * o + N_TILE * h
+                nc.sync.dma_start(out=out[:, first : first + N_TILE], in_=result[:])

@@ -58,25 +58,31 @@ def tile_quaternionlinear_w_kernel(
         identity = const.tile([P, P], F32)
         make_identity(nc, identity[:])
 
-        x_rows_of = []
-        for c in range(C):
-            x_rows = x_pool.tile([P, QI], BF16)
-            nc.sync.dma_start(out=x_rows[:], in_=x[:, QI * c : QI * (c + 1)])
-            x_rows_of.append(x_rows)
-
         planes_of = []
         for w in range(C):
             planes = plane_pool.tile([P, QO], U8, align_bytes=64)
             nc.vector.memset(planes[:].bitcast(I32), 0)
             planes_of.append(planes)
 
-        w_codes_of = {}
-        for w in range(C):
+        def load_scales(w):
             for quadrant in range(4):
                 nc.sync.dma_start(
                     out=planes_of[w][32 * quadrant : 32 * quadrant + 16, :].bitcast(I32),
                     in_=scales_in[w][:, 4 * quadrant : 4 * quadrant + 4, :].bitcast(I32),
                 )
+
+        load_scales(0)
+
+        x_rows_of = []
+        for c in range(C):
+            x_rows = x_pool.tile([P, QI], BF16)
+            nc.sync.dma_start(out=x_rows[:], in_=x[:, QI * c : QI * (c + 1)])
+            x_rows_of.append(x_rows)
+
+        w_codes_of = {}
+        for w in range(C):
+            if w + 1 < C:
+                load_scales(w + 1)
             for g in range(G):
                 w_codes = weight_pool.tile([P, QO], U32, align_bytes=64)
                 nc.sync.dma_start(

@@ -30,6 +30,7 @@ HAMILTON = (
     ((3, MINUS), (2, PLUS), (1, MINUS), (0, PLUS)),
 )
 SQUARE = 32
+TAIL_PIECES = 2
 
 
 def tile_quaternionlinear_w_kernel(
@@ -58,21 +59,6 @@ def tile_quaternionlinear_w_kernel(
         identity = const.tile([P, P], F32)
         make_identity(nc, identity[:])
 
-        planes_of = []
-        for w in range(C):
-            planes = plane_pool.tile([P, QO], U8, align_bytes=64)
-            nc.vector.memset(planes[:].bitcast(I32), 0)
-            planes_of.append(planes)
-
-        def load_scales(w):
-            for quadrant in range(4):
-                nc.sync.dma_start(
-                    out=planes_of[w][32 * quadrant : 32 * quadrant + 16, :].bitcast(I32),
-                    in_=scales_in[w][:, 4 * quadrant : 4 * quadrant + 4, :].bitcast(I32),
-                )
-
-        load_scales(0)
-
         x_rows_of = []
         for c in range(C):
             x_rows = x_pool.tile([P, QI], BF16)
@@ -81,8 +67,6 @@ def tile_quaternionlinear_w_kernel(
 
         w_codes_of = {}
         for w in range(C):
-            if w + 1 < C:
-                load_scales(w + 1)
             for g in range(G):
                 w_codes = weight_pool.tile([P, QO], U32, align_bytes=64)
                 nc.sync.dma_start(
@@ -90,6 +74,17 @@ def tile_quaternionlinear_w_kernel(
                     in_=words_in[w][g].rearrange("p n t -> p (n t)").bitcast(I32),
                 )
                 w_codes_of[(w, g)] = w_codes
+
+        planes_of = []
+        for w in range(C):
+            planes = plane_pool.tile([P, QO], U8, align_bytes=64)
+            nc.vector.memset(planes[:].bitcast(I32), 0)
+            for quadrant in range(4):
+                nc.gpsimd.dma_start(
+                    out=planes[32 * quadrant : 32 * quadrant + 16, :].bitcast(F32),
+                    in_=scales_in[w][:, 4 * quadrant : 4 * quadrant + 4, :].bitcast(F32),
+                )
+            planes_of.append(planes)
 
         folded = const.tile([P, C, SQUARE], BF16)
         for w in range(C):
@@ -175,42 +170,48 @@ def tile_quaternionlinear_w_kernel(
             nc.vector.transpose(out=bias[:], in_=repeated[:].rearrange("p b j -> p (b j)"))
             bias_of.append(bias)
 
-        acc_of = {}
-        for o in range(C):
-            for h in range(H):
-                acc = psum.tile([P, N_TILE], F32, tag="bank")
-                acc_of[(o, h)] = acc
-
-        def one_pass(o, h, w, g):
+        def one_pass(acc, o, first, width, w, g):
             c = [HAMILTON[row][o][0] for row in range(C)].index(w)
             copy_of_x = HAMILTON[c][o][1]
             nc.tensor.matmul_mx(
-                out=acc_of[(o, h)][:],
+                out=acc[:],
                 lhsT=x_codes_of[c][:, copy_of_x, g, :].bitcast(FP8X4),
                 lhsT_scale=x_scales_of[c][:, copy_of_x, g, :],
-                rhs=w_codes_of[(w, g)][:, N_TILE * h : N_TILE * (h + 1)].bitcast(FP8X4),
-                rhs_scale=planes_of[w][PACK * g : P, N_TILE * h : N_TILE * (h + 1)],
+                rhs=w_codes_of[(w, g)][:, first : first + width].bitcast(FP8X4),
+                rhs_scale=planes_of[w][PACK * g : P, first : first + width],
                 start=(w == 0 and g == 0),
                 stop=(w == C - 1 and g == G - 1),
             )
 
+        def finish(acc, o, first, width):
+            result = stage.tile([P, width], F32, tag="result")
+            in_bias = QO * (o % 2) + first
+            nc.vector.tensor_tensor(
+                out=result[:], in0=acc[:], in1=bias_of[o // 2][:, in_bias : in_bias + width], op=add
+            )
+            nc.sync.dma_start(out=out[:, QO * o + first : QO * o + first + width], in_=result[:])
+
+        swept = [(o, N_TILE * h) for o in range(C) for h in range(H)][:-1]
+        acc_of = {}
+        for o, first in swept:
+            acc = psum.tile([P, N_TILE], F32, tag="bank")
+            acc_of[(o, first)] = acc
+
         for w in range(C - 1):
             for g in range(G):
-                for o in range(C):
-                    for h in range(H):
-                        one_pass(o, h, w, g)
+                for o, first in swept:
+                    one_pass(acc_of[(o, first)], o, first, N_TILE, w, g)
 
-        for o in range(C):
-            for h in range(H):
+        for o, first in swept:
+            for g in range(G):
+                one_pass(acc_of[(o, first)], o, first, N_TILE, C - 1, g)
+            finish(acc_of[(o, first)], o, first, N_TILE)
+
+        width = N_TILE // TAIL_PIECES
+        for piece in range(TAIL_PIECES):
+            first = QO - N_TILE + width * piece
+            acc = psum.tile([P, width], F32, tag="bank")
+            for w in range(C):
                 for g in range(G):
-                    one_pass(o, h, C - 1, g)
-                result = stage.tile([P, N_TILE], F32)
-                in_bias = QO * (o % 2) + N_TILE * h
-                nc.vector.tensor_tensor(
-                    out=result[:],
-                    in0=acc_of[(o, h)][:],
-                    in1=bias_of[o // 2][:, in_bias : in_bias + N_TILE],
-                    op=add,
-                )
-                first = QO * o + N_TILE * h
-                nc.sync.dma_start(out=out[:, first : first + N_TILE], in_=result[:])
+                    one_pass(acc, C - 1, first, width, w, g)
+            finish(acc, C - 1, first, width)

@@ -30,6 +30,8 @@ HAMILTON = (
     ((3, MINUS), (2, PLUS), (1, MINUS), (0, PLUS)),
 )
 SQUARE = 32
+WARM_UP = 5
+BETWEEN_RUNS = 2
 TAIL_PIECES = 2
 
 
@@ -58,6 +60,16 @@ def tile_quaternionlinear_w_kernel(
 
         identity = const.tile([P, P], F32)
         make_identity(nc, identity[:])
+
+        zeros = const.tile([P, N_TILE], BF16)
+        nc.vector.memset(zeros[:], 0.0)
+        idle_bank = psum.tile([P, N_TILE], F32, tag="bank")
+
+        def keep_busy(times):
+            for i in range(times):
+                nc.tensor.matmul(idle_bank[:], lhsT=zeros[:, 0:P], rhs=zeros[:], start=True, stop=True)
+
+        keep_busy(WARM_UP)
 
         x_rows_of = []
         for c in range(C):
@@ -131,6 +143,8 @@ def tile_quaternionlinear_w_kernel(
             x_codes_of.append(x_codes)
             x_scales_of.append(x_scales)
             quantise(c, PLUS)
+            if c == 1:
+                keep_busy(BETWEEN_RUNS)
 
         for c in range(1, C):
             minus = x_pool.tile([P, G, P, PACK], BF16, align_bytes=64)

@@ -20,6 +20,8 @@ G = QI // K_PASS
 N_TILE = 512
 H = QO // N_TILE
 PLUS, MINUS = 0, 1
+SQUARE = 32
+QUADRANTS = P // SQUARE
 
 FLOPS = 2 * P * (C * QI) * (C * QO)
 
@@ -29,9 +31,9 @@ HAMILTON = (
     ((2, MINUS), (3, MINUS), (0, PLUS), (1, PLUS)),
     ((3, MINUS), (2, PLUS), (1, MINUS), (0, PLUS)),
 )
-SQUARE = 32
+EARLY_GROUPS = (0, 1)
+LATE_GROUPS = (2, 3)
 WARM_UP = 5
-BETWEEN_RUNS = 2
 TAIL_PIECES = 2
 
 
@@ -50,7 +52,8 @@ def tile_quaternionlinear_w_kernel(
 
     with ExitStack() as ctx:
         const = ctx.enter_context(tc.tile_pool(name="const", bufs=1))
-        x_pool = ctx.enter_context(tc.tile_pool(name="x_pool", bufs=C))
+        x_pool = ctx.enter_context(tc.tile_pool(name="x_pool", bufs=G))
+        late_pool = ctx.enter_context(tc.tile_pool(name="late_pool", bufs=len(LATE_GROUPS)))
         plane_pool = ctx.enter_context(tc.tile_pool(name="plane_pool", bufs=C))
         weight_pool = ctx.enter_context(tc.tile_pool(name="weight_pool", bufs=C * G))
         bias_pool = ctx.enter_context(tc.tile_pool(name="bias_pool", bufs=2))
@@ -58,46 +61,23 @@ def tile_quaternionlinear_w_kernel(
         psum = ctx.enter_context(tc.psum_pool(name="psum", bufs=8))
         ctx.enter_context(tc.manual_schedule())
 
-        identity = const.tile([P, P], F32)
-        make_identity(nc, identity[:])
-
-        zeros = const.tile([P, N_TILE], BF16)
-        nc.vector.memset(zeros[:], 0.0)
-        idle_bank = psum.tile([P, N_TILE], F32, tag="bank")
-
-        def keep_busy(times):
-            for i in range(times):
-                nc.tensor.matmul(idle_bank[:], lhsT=zeros[:, 0:P], rhs=zeros[:], start=True, stop=True)
-
-        keep_busy(WARM_UP)
-
-        x_rows_of = []
-        for c in range(C):
-            x_rows = x_pool.tile([P, QI], BF16)
-            nc.sync.dma_start(out=x_rows[:], in_=x[:, QI * c : QI * (c + 1)])
-            x_rows_of.append(x_rows)
-
-        w_codes_of = {}
-        for w in range(C):
-            for g in range(G):
-                w_codes = weight_pool.tile([P, QO], U32, align_bytes=64)
-                nc.sync.dma_start(
-                    out=w_codes[:].bitcast(I32),
-                    in_=words_in[w][g].rearrange("p n t -> p (n t)").bitcast(I32),
-                )
-                w_codes_of[(w, g)] = w_codes
-
         planes_of = []
         for w in range(C):
             planes = plane_pool.tile([P, QO], U8, align_bytes=64)
             nc.vector.memset(planes[:].bitcast(I32), 0)
-            for quadrant in range(4):
-                nc.gpsimd.dma_start(
-                    out=planes[32 * quadrant : 32 * quadrant + 16, :].bitcast(F32),
-                    in_=scales_in[w][:, 4 * quadrant : 4 * quadrant + 4, :].bitcast(F32),
-                )
             planes_of.append(planes)
 
+        def load_planes(w):
+            for quadrant in range(QUADRANTS):
+                nc.gpsimd.dma_start(
+                    out=planes_of[w][SQUARE * quadrant : SQUARE * quadrant + 16, :].bitcast(F32),
+                    in_=scales_in[w][:, 4 * quadrant : 4 * quadrant + 4, :].bitcast(F32),
+                )
+
+        identity = const.tile([P, P], F32)
+        make_identity(nc, identity[:])
+        for w in range(C):
+            load_planes(w)
         folded = const.tile([P, C, SQUARE], BF16)
         for w in range(C):
             nc.gpsimd.dma_start(
@@ -105,56 +85,141 @@ def tile_quaternionlinear_w_kernel(
                 in_=bias_in[w]
                 .rearrange("(a i) -> a i", i=SQUARE)
                 .unsqueeze(0)
-                .to_broadcast([P // SQUARE, SQUARE, SQUARE]),
+                .to_broadcast([QUADRANTS, SQUARE, SQUARE]),
             )
+
+        by_group = x.rearrange("m (c g k) -> m c g k", c=C, g=G)
+        by_quadrant = x.rearrange("m (c g q e) -> m c g q e", c=C, g=G, q=QUADRANTS)
+
+        x_rows_of = {}
+
+        def load_rows(g, pair):
+            x_rows = x_pool.tile([P, 2, K_PASS], BF16)
+            nc.sync.dma_start(out=x_rows[:], in_=by_group[:, 2 * pair : 2 * pair + 2, g, :])
+            x_rows_of[(g, pair)] = x_rows
+
+        by_square_of = {}
+
+        def load_squares(g, block):
+            for quadrant in range(QUADRANTS):
+                nc.sync.dma_start(
+                    out=by_square_of[g][SQUARE * quadrant : SQUARE * (quadrant + 1), :, block, :],
+                    in_=by_quadrant[SQUARE * block : SQUARE * (block + 1), :, g, quadrant, :],
+                )
+
+        w_codes_of = {}
+
+        def load_weights(w, g, pieces=1):
+            w_codes = weight_pool.tile([P, QO], U32, align_bytes=64)
+            width = QO // pieces
+            for piece in range(pieces):
+                nc.sync.dma_start(
+                    out=w_codes[:, width * piece : width * (piece + 1)].bitcast(I32),
+                    in_=words_in[w][g]
+                    .rearrange("p n t -> p (n t)")[:, PACK * width * piece : PACK * width * (piece + 1)]
+                    .bitcast(I32),
+                )
+            w_codes_of[(w, g)] = w_codes
+
+        for g in LATE_GROUPS:
+            by_square = late_pool.tile([P, C, QUADRANTS, P], BF16, align_bytes=64)
+            by_square_of[g] = by_square
+
+        for g in EARLY_GROUPS:
+            for pair in range(C // 2):
+                load_rows(g, pair)
+        load_weights(0, 0, pieces=H)
+        load_weights(0, 1)
+        woven = [(g, block) for g in LATE_GROUPS for block in range(QUADRANTS)]
+        remaining = [(w, g) for w in range(1, C) for g in EARLY_GROUPS] + [
+            (w, g) for g in LATE_GROUPS for w in range(C)
+        ]
+        for n, (w, g) in enumerate(remaining):
+            load_weights(w, g)
+            if n < len(woven):
+                load_squares(woven[n][0], woven[n][1])
+
+        zeros = const.tile([P, N_TILE], BF16)
+        nc.vector.memset(zeros[:], 0.0)
+        unread = const.tile([P, 1], BF16)
+        nc.scalar.copy(out=unread[:], in_=zeros[:, 0:1])
+        idle_bank = psum.tile([P, N_TILE], F32, tag="bank")
+        for i in range(WARM_UP):
+            nc.tensor.matmul(idle_bank[:], lhsT=zeros[:, 0:P], rhs=zeros[:], start=True, stop=True)
 
         grouped_of = {}
-        x_codes_of = []
-        x_scales_of = []
+        x_codes_of = {}
+        x_scales_of = {}
+        for g in range(G):
+            plus = x_pool.tile([P, C, P, PACK], BF16, align_bytes=64)
+            minus = x_pool.tile([P, C, P, PACK], BF16, align_bytes=64)
+            x_codes = x_pool.tile([P, 2, C, P], U32, align_bytes=64)
+            x_scales = x_pool.tile([P, 2, C, P], U8, align_bytes=64)
+            grouped_of[(g, PLUS)] = plus
+            grouped_of[(g, MINUS)] = minus
+            x_codes_of[g] = x_codes
+            x_scales_of[g] = x_scales
 
-        def quantise(c, copy_of_x):
+        def quantise(g, copy_of_x, first, count):
             nc.vector.quantize_mx(
-                out=x_codes_of[c][:, copy_of_x].rearrange("p g m -> p (g m)").bitcast(FP8X4),
-                scales=x_scales_of[c][:, copy_of_x].rearrange("p g m -> p (g m)"),
-                in_=grouped_of[(c, copy_of_x)][:].rearrange("p g m t -> p (g m t)"),
+                out=x_codes_of[g][:, copy_of_x, first : first + count, :]
+                .rearrange("p c m -> p (c m)")
+                .bitcast(FP8X4),
+                scales=x_scales_of[g][:, copy_of_x, first : first + count, :].rearrange("p c m -> p (c m)"),
+                in_=grouped_of[(g, copy_of_x)][:, first : first + count, :, :].rearrange(
+                    "p c m t -> p (c m t)"
+                ),
             )
 
-        for c in range(C):
-            x_words = x_rows_of[c][:].bitcast(F32)
-            words_in_group = K_PASS // 2
-            plus = x_pool.tile([P, G, P, PACK], BF16, align_bytes=64)
-            for pair in range(G // 2):
+        def negate(g):
+            nc.vector.tensor_scalar_mul(
+                out=grouped_of[(g, MINUS)][:].rearrange("p c m t -> p (c m t)"),
+                in0=grouped_of[(g, PLUS)][:].rearrange("p c m t -> p (c m t)"),
+                scalar1=-1.0,
+            )
+
+        for g in EARLY_GROUPS:
+            for pair in range(C // 2):
+                x_words = x_rows_of[(g, pair)][:].rearrange("p c k -> p (c k)").bitcast(F32)
+                words_in_group = K_PASS // 2
                 flipped = psum.tile([P, 2, 2, P], F32, tag="bank")
                 for j in range(2):
-                    g = 2 * pair + j
                     for u in range(2):
                         nc.tensor.transpose(
                             flipped[:, j, u, :],
-                            x_words[:, words_in_group * g + u : words_in_group * (g + 1) : 2],
+                            x_words[:, words_in_group * j + u : words_in_group * (j + 1) : 2],
                             identity[:],
                         )
                 nc.scalar.copy(
-                    out=plus[:, 2 * pair : 2 * pair + 2, :, :].bitcast(F32),
+                    out=grouped_of[(g, PLUS)][:, 2 * pair : 2 * pair + 2, :, :].bitcast(F32),
                     in_=flipped[:].rearrange("p j u m -> p j m u"),
                 )
-            grouped_of[(c, PLUS)] = plus
-            x_codes = x_pool.tile([P, 2, G, P], U32, align_bytes=64)
-            x_scales = x_pool.tile([P, 2, G, P], U8, align_bytes=64)
-            x_codes_of.append(x_codes)
-            x_scales_of.append(x_scales)
-            quantise(c, PLUS)
-            if c == 1:
-                keep_busy(BETWEEN_RUNS)
+                quantise(g, PLUS, 2 * pair, 2)
+        for g in EARLY_GROUPS:
+            negate(g)
+        for g in EARLY_GROUPS:
+            quantise(g, MINUS, 0, C)
 
-        for c in range(1, C):
-            minus = x_pool.tile([P, G, P, PACK], BF16, align_bytes=64)
-            nc.vector.tensor_scalar_mul(
-                out=minus[:].rearrange("p g m t -> p (g m t)"),
-                in0=grouped_of[(c, PLUS)][:].rearrange("p g m t -> p (g m t)"),
-                scalar1=-1.0,
+        def turn_late_group(g):
+            words = by_square_of[g][:].rearrange("p c b e -> p (c b e)").bitcast(F32)
+            sorted_words = late_pool.tile([P, C * QUADRANTS, 2, SQUARE], F32, align_bytes=64)
+            nc.scalar.copy(
+                out=sorted_words[:], in_=words.rearrange("p (b i u) -> p b u i", i=SQUARE, u=2)
             )
-            grouped_of[(c, MINUS)] = minus
-            quantise(c, MINUS)
+            turned = late_pool.tile([P, C * QUADRANTS * 2 * SQUARE], F32, align_bytes=64)
+            nc.vector.transpose(out=turned[:], in_=sorted_words[:].rearrange("p b u i -> p (b u i)"))
+            nc.scalar.copy(
+                out=grouped_of[(g, PLUS)][:]
+                .rearrange("p c m t -> p (c m t)")
+                .bitcast(F32)
+                .rearrange("p (b j u) -> p b j u", j=SQUARE, u=2),
+                in_=turned[:].rearrange("p (b u j) -> p b j u", u=2, j=SQUARE),
+            )
+            quantise(g, PLUS, 0, C)
+            negate(g)
+            quantise(g, MINUS, 0, C)
+
+        turn_late_group(LATE_GROUPS[0])
 
         r_minus_k = const.tile([P, SQUARE], F32)
         r_plus_k = const.tile([P, SQUARE], F32)
@@ -171,6 +236,9 @@ def tile_quaternionlinear_w_kernel(
         nc.vector.tensor_tensor(out=combined[:, 3, :], in0=r_plus_k[:], in1=i_minus_j[:], op=add)
         upright = const.tile([P, C * SQUARE], F32, align_bytes=64)
         nc.vector.transpose(out=upright[:], in_=combined[:].rearrange("p o i -> p (o i)"))
+
+        turn_late_group(LATE_GROUPS[1])
+
         bias_of = []
         for s in range(2):
             repeated = bias_pool.tile([P, 2 * SQUARE, SQUARE], F32, align_bytes=64)
@@ -184,17 +252,17 @@ def tile_quaternionlinear_w_kernel(
             nc.vector.transpose(out=bias[:], in_=repeated[:].rearrange("p b j -> p (b j)"))
             bias_of.append(bias)
 
-        def one_pass(acc, o, first, width, w, g):
+        def one_pass(acc, o, first, width, w, g, start, stop):
             c = [HAMILTON[row][o][0] for row in range(C)].index(w)
             copy_of_x = HAMILTON[c][o][1]
             nc.tensor.matmul_mx(
                 out=acc[:],
-                lhsT=x_codes_of[c][:, copy_of_x, g, :].bitcast(FP8X4),
-                lhsT_scale=x_scales_of[c][:, copy_of_x, g, :],
+                lhsT=x_codes_of[g][:, copy_of_x, c, :].bitcast(FP8X4),
+                lhsT_scale=x_scales_of[g][:, copy_of_x, c, :],
                 rhs=w_codes_of[(w, g)][:, first : first + width].bitcast(FP8X4),
                 rhs_scale=planes_of[w][PACK * g : P, first : first + width],
-                start=(w == 0 and g == 0),
-                stop=(w == C - 1 and g == G - 1),
+                start=start,
+                stop=stop,
             )
 
         def finish(acc, o, first, width):
@@ -205,27 +273,28 @@ def tile_quaternionlinear_w_kernel(
             )
             nc.sync.dma_start(out=out[:, QO * o + first : QO * o + first + width], in_=result[:])
 
-        swept = [(o, N_TILE * h) for o in range(C) for h in range(H)][:-1]
+        swept = [(o, N_TILE * h) for h in range(H) for o in range(C)][:-1]
         acc_of = {}
         for o, first in swept:
             acc = psum.tile([P, N_TILE], F32, tag="bank")
             acc_of[(o, first)] = acc
 
-        for w in range(C - 1):
-            for g in range(G):
-                for o, first in swept:
-                    one_pass(acc_of[(o, first)], o, first, N_TILE, w, g)
+        arrival = [(w, g) for w in range(C) for g in EARLY_GROUPS] + [
+            (w, g) for g in LATE_GROUPS for w in range(C)
+        ]
+        for w, g in arrival[: -C]:
+            for o, first in swept:
+                one_pass(acc_of[(o, first)], o, first, N_TILE, w, g, (w, g) == arrival[0], False)
 
         for o, first in swept:
-            for g in range(G):
-                one_pass(acc_of[(o, first)], o, first, N_TILE, C - 1, g)
+            for w, g in arrival[-C:]:
+                one_pass(acc_of[(o, first)], o, first, N_TILE, w, g, False, (w, g) == arrival[-1])
             finish(acc_of[(o, first)], o, first, N_TILE)
 
         width = N_TILE // TAIL_PIECES
         for piece in range(TAIL_PIECES):
             first = QO - N_TILE + width * piece
             acc = psum.tile([P, width], F32, tag="bank")
-            for w in range(C):
-                for g in range(G):
-                    one_pass(acc, C - 1, first, width, w, g)
+            for w, g in arrival:
+                one_pass(acc, C - 1, first, width, w, g, (w, g) == arrival[0], (w, g) == arrival[-1])
             finish(acc, C - 1, first, width)

@@ -61,23 +61,8 @@ def tile_quaternionlinear_w_kernel(
         psum = ctx.enter_context(tc.psum_pool(name="psum", bufs=8))
         ctx.enter_context(tc.manual_schedule())
 
-        planes_of = []
-        for w in range(C):
-            planes = plane_pool.tile([P, QO], U8, align_bytes=64)
-            nc.vector.memset(planes[:].bitcast(I32), 0)
-            planes_of.append(planes)
-
-        def load_planes(w):
-            for quadrant in range(QUADRANTS):
-                nc.gpsimd.dma_start(
-                    out=planes_of[w][SQUARE * quadrant : SQUARE * quadrant + 16, :].bitcast(F32),
-                    in_=scales_in[w][:, 4 * quadrant : 4 * quadrant + 4, :].bitcast(F32),
-                )
-
         identity = const.tile([P, P], F32)
         make_identity(nc, identity[:])
-        for w in range(C):
-            load_planes(w)
         folded = const.tile([P, C, SQUARE], BF16)
         for w in range(C):
             nc.gpsimd.dma_start(
@@ -87,6 +72,19 @@ def tile_quaternionlinear_w_kernel(
                 .unsqueeze(0)
                 .to_broadcast([QUADRANTS, SQUARE, SQUARE]),
             )
+
+        planes_of = []
+        for w in range(C):
+            planes = plane_pool.tile([P, QO], U8, align_bytes=64)
+            nc.vector.memset(planes[:].bitcast(I32), 0)
+            planes_of.append(planes)
+
+        def load_planes(w):
+            for quadrant in range(QUADRANTS):
+                nc.sync.dma_start(
+                    out=planes_of[w][SQUARE * quadrant : SQUARE * quadrant + 16, :].bitcast(I32),
+                    in_=scales_in[w][:, 4 * quadrant : 4 * quadrant + 4, :].bitcast(I32),
+                )
 
         by_group = x.rearrange("m (c g k) -> m c g k", c=C, g=G)
         by_quadrant = x.rearrange("m (c g q e) -> m c g q e", c=C, g=G, q=QUADRANTS)
@@ -128,6 +126,7 @@ def tile_quaternionlinear_w_kernel(
         for g in EARLY_GROUPS:
             for pair in range(C // 2):
                 load_rows(g, pair)
+        load_planes(0)
         load_weights(0, 0, pieces=H)
         load_weights(0, 1)
         woven = [(g, block) for g in LATE_GROUPS for block in range(QUADRANTS)]
@@ -135,6 +134,8 @@ def tile_quaternionlinear_w_kernel(
             (w, g) for g in LATE_GROUPS for w in range(C)
         ]
         for n, (w, g) in enumerate(remaining):
+            if g == EARLY_GROUPS[0]:
+                load_planes(w)
             load_weights(w, g)
             if n < len(woven):
                 load_squares(woven[n][0], woven[n][1])
@@ -219,8 +220,6 @@ def tile_quaternionlinear_w_kernel(
             negate(g)
             quantise(g, MINUS, 0, C)
 
-        turn_late_group(LATE_GROUPS[0])
-
         r_minus_k = const.tile([P, SQUARE], F32)
         r_plus_k = const.tile([P, SQUARE], F32)
         i_plus_j = const.tile([P, SQUARE], F32)
@@ -237,8 +236,6 @@ def tile_quaternionlinear_w_kernel(
         upright = const.tile([P, C * SQUARE], F32, align_bytes=64)
         nc.vector.transpose(out=upright[:], in_=combined[:].rearrange("p o i -> p (o i)"))
 
-        turn_late_group(LATE_GROUPS[1])
-
         bias_of = []
         for s in range(2):
             repeated = bias_pool.tile([P, 2 * SQUARE, SQUARE], F32, align_bytes=64)
@@ -251,6 +248,9 @@ def tile_quaternionlinear_w_kernel(
             bias = bias_pool.tile([P, 2 * QO], F32, align_bytes=64)
             nc.vector.transpose(out=bias[:], in_=repeated[:].rearrange("p b j -> p (b j)"))
             bias_of.append(bias)
+
+        for g in LATE_GROUPS:
+            turn_late_group(g)
 
         def one_pass(acc, o, first, width, w, g, start, stop):
             c = [HAMILTON[row][o][0] for row in range(C)].index(w)

@@ -34,7 +34,7 @@ HAMILTON = (
 EARLY_GROUPS = (0, 1)
 LATE_GROUPS = (2, 3)
 WARM_UP = 5
-TAIL_PIECES = 2
+BANK_BY_BANK = 2
 
 
 def tile_quaternionlinear_w_kernel(
@@ -273,7 +273,7 @@ def tile_quaternionlinear_w_kernel(
             )
             nc.sync.dma_start(out=out[:, QO * o + first : QO * o + first + width], in_=result[:])
 
-        swept = [(o, N_TILE * h) for h in range(H) for o in range(C)][:-1]
+        swept = [(o, N_TILE * h) for h in range(H) for o in range(C)]
         acc_of = {}
         for o, first in swept:
             acc = psum.tile([P, N_TILE], F32, tag="bank")
@@ -282,19 +282,11 @@ def tile_quaternionlinear_w_kernel(
         arrival = [(w, g) for w in range(C) for g in EARLY_GROUPS] + [
             (w, g) for g in LATE_GROUPS for w in range(C)
         ]
-        for w, g in arrival[: -C]:
+        for w, g in arrival[:-BANK_BY_BANK]:
             for o, first in swept:
                 one_pass(acc_of[(o, first)], o, first, N_TILE, w, g, (w, g) == arrival[0], False)
 
         for o, first in swept:
-            for w, g in arrival[-C:]:
+            for w, g in arrival[-BANK_BY_BANK:]:
                 one_pass(acc_of[(o, first)], o, first, N_TILE, w, g, False, (w, g) == arrival[-1])
             finish(acc_of[(o, first)], o, first, N_TILE)
-
-        width = N_TILE // TAIL_PIECES
-        for piece in range(TAIL_PIECES):
-            first = QO - N_TILE + width * piece
-            acc = psum.tile([P, width], F32, tag="bank")
-            for w, g in arrival:
-                one_pass(acc, C - 1, first, width, w, g, (w, g) == arrival[0], (w, g) == arrival[-1])
-            finish(acc, C - 1, first, width)

@@ -34,7 +34,7 @@ HAMILTON = (
 EARLY_GROUPS = (0, 1)
 LATE_GROUPS = (2, 3)
 WARM_UP = 5
-BANK_BY_BANK = 2
+BANK_BY_BANK = 3
 
 
 def tile_quaternionlinear_w_kernel(
@@ -57,7 +57,7 @@ def tile_quaternionlinear_w_kernel(
         plane_pool = ctx.enter_context(tc.tile_pool(name="plane_pool", bufs=C))
         weight_pool = ctx.enter_context(tc.tile_pool(name="weight_pool", bufs=C * G))
         bias_pool = ctx.enter_context(tc.tile_pool(name="bias_pool", bufs=2))
-        stage = ctx.enter_context(tc.tile_pool(name="stage", bufs=4))
+        stage = ctx.enter_context(tc.tile_pool(name="stage", bufs=C * H))
         psum = ctx.enter_context(tc.psum_pool(name="psum", bufs=8))
         ctx.enter_context(tc.manual_schedule())
 

@@ -75,7 +75,7 @@ def tile_quaternionlinear_w_kernel(
 
         planes_of = []
         for w in range(C):
-            planes = plane_pool.tile([P, QO], U8, align_bytes=64)
+            planes = plane_pool.tile([P, QO], U8, align_bytes=256)
             nc.vector.memset(planes[:].bitcast(I32), 0)
             planes_of.append(planes)
 
@@ -108,7 +108,7 @@ def tile_quaternionlinear_w_kernel(
         w_codes_of = {}
 
         def load_weights(w, g, pieces=1):
-            w_codes = weight_pool.tile([P, QO], U32, align_bytes=64)
+            w_codes = weight_pool.tile([P, QO], U32, align_bytes=256)
             width = QO // pieces
             for piece in range(pieces):
                 nc.sync.dma_start(
@@ -154,8 +154,8 @@ def tile_quaternionlinear_w_kernel(
         for g in range(G):
             plus = x_pool.tile([P, C, P, PACK], BF16, align_bytes=64)
             minus = x_pool.tile([P, C, P, PACK], BF16, align_bytes=64)
-            x_codes = x_pool.tile([P, 2, C, P], U32, align_bytes=64)
-            x_scales = x_pool.tile([P, 2, C, P], U8, align_bytes=64)
+            x_codes = x_pool.tile([P, 2, C, P], U32, align_bytes=256)
+            x_scales = x_pool.tile([P, 2, C, P], U8, align_bytes=256)
             grouped_of[(g, PLUS)] = plus
             grouped_of[(g, MINUS)] = minus
             x_codes_of[g] = x_codes

from contextlib import ExitStack

import concourse.mybir as mybir
from concourse.masks import make_identity

F32 = mybir.dt.float32
BF16 = mybir.dt.bfloat16
I32 = mybir.dt.int32
U32 = mybir.dt.uint32
U8 = mybir.dt.uint8
FP8X4 = mybir.dt.float8_e4m3fn_x4

P = 128
PACK = 4
K_PASS = P * PACK
C = 4
QI = 2048
QO = 1024
G = QI // K_PASS
N_TILE = 512
H = QO // N_TILE
PLUS, MINUS = 0, 1
SQUARE = 32
QUADRANTS = P // SQUARE

FLOPS = 2 * P * (C * QI) * (C * QO)

HAMILTON = (
    ((0, PLUS), (1, PLUS), (2, PLUS), (3, PLUS)),
    ((1, MINUS), (0, PLUS), (3, PLUS), (2, MINUS)),
    ((2, MINUS), (3, MINUS), (0, PLUS), (1, PLUS)),
    ((3, MINUS), (2, PLUS), (1, MINUS), (0, PLUS)),
)
EARLY_GROUPS = (0, 1)
LATE_GROUPS = (2, 3)
WARM_UP = 5
BANK_BY_BANK = 3


def tile_quaternionlinear_w_kernel(
    tc, x,
    Wr_words, Wr_scales, Wi_words, Wi_scales, Wj_words, Wj_scales, Wk_words, Wk_scales,
    br, bi, bj, bk,
    out,
):
    nc = tc.nc
    words_in = (Wr_words, Wi_words, Wj_words, Wk_words)
    scales_in = (Wr_scales, Wi_scales, Wj_scales, Wk_scales)
    bias_in = (br, bi, bj, bk)
    add = mybir.AluOpType.add
    subtract = mybir.AluOpType.subtract

    with ExitStack() as ctx:
        const = ctx.enter_context(tc.tile_pool(name="const", bufs=1))
        x_pool = ctx.enter_context(tc.tile_pool(name="x_pool", bufs=G))
        late_pool = ctx.enter_context(tc.tile_pool(name="late_pool", bufs=len(LATE_GROUPS)))
        plane_pool = ctx.enter_context(tc.tile_pool(name="plane_pool", bufs=C))
        weight_pool = ctx.enter_context(tc.tile_pool(name="weight_pool", bufs=C * G))
        bias_pool = ctx.enter_context(tc.tile_pool(name="bias_pool", bufs=2))
        stage = ctx.enter_context(tc.tile_pool(name="stage", bufs=C * H))
        psum = ctx.enter_context(tc.psum_pool(name="psum", bufs=8))
        ctx.enter_context(tc.manual_schedule())

        identity = const.tile([P, P], F32)
        make_identity(nc, identity[:])
        folded = const.tile([P, C, SQUARE], BF16)
        for w in range(C):
            nc.gpsimd.dma_start(
                out=folded[:, w, :],
                in_=bias_in[w]
                .rearrange("(a i) -> a i", i=SQUARE)
                .unsqueeze(0)
                .to_broadcast([QUADRANTS, SQUARE, SQUARE]),
            )

        planes_of = []
        for w in range(C):
            planes = plane_pool.tile([P, QO], U8, align_bytes=256)
            nc.vector.memset(planes[:].bitcast(I32), 0)
            planes_of.append(planes)

        def load_planes(w):
            for quadrant in range(QUADRANTS):
                nc.sync.dma_start(
                    out=planes_of[w][SQUARE * quadrant : SQUARE * quadrant + 16, :].bitcast(I32),
                    in_=scales_in[w][:, 4 * quadrant : 4 * quadrant + 4, :].bitcast(I32),
                )

        by_group = x.rearrange("m (c g k) -> m c g k", c=C, g=G)
        by_quadrant = x.rearrange("m (c g q e) -> m c g q e", c=C, g=G, q=QUADRANTS)

        x_rows_of = {}

        def load_rows(g, pair):
            x_rows = x_pool.tile([P, 2, K_PASS], BF16)
            nc.sync.dma_start(out=x_rows[:], in_=by_group[:, 2 * pair : 2 * pair + 2, g, :])
            x_rows_of[(g, pair)] = x_rows

        by_square_of = {}

        def load_squares(g, block):
            for quadrant in range(QUADRANTS):
                nc.sync.dma_start(
                    out=by_square_of[g][SQUARE * quadrant : SQUARE * (quadrant + 1), :, block, :],
                    in_=by_quadrant[SQUARE * block : SQUARE * (block + 1), :, g, quadrant, :],
                )

        w_codes_of = {}

        def load_weights(w, g, pieces=1):
            w_codes = weight_pool.tile([P, QO], U32, align_bytes=256)
            width = QO // pieces
            for piece in range(pieces):
                nc.sync.dma_start(
                    out=w_codes[:, width * piece : width * (piece + 1)].bitcast(I32),
                    in_=words_in[w][g]
                    .rearrange("p n t -> p (n t)")[:, PACK * width * piece : PACK * width * (piece + 1)]
                    .bitcast(I32),
                )
            w_codes_of[(w, g)] = w_codes

        for g in LATE_GROUPS:
            by_square = late_pool.tile([P, C, QUADRANTS, P], BF16, align_bytes=64)
            by_square_of[g] = by_square

        for g in EARLY_GROUPS:
            for pair in range(C // 2):
                load_rows(g, pair)
        load_planes(0)
        load_weights(0, 0, pieces=H)
        load_weights(0, 1)
        woven = [(g, block) for g in LATE_GROUPS for block in range(QUADRANTS)]
        remaining = [(w, g) for w in range(1, C) for g in EARLY_GROUPS] + [
            (w, g) for g in LATE_GROUPS for w in range(C)
        ]
        for n, (w, g) in enumerate(remaining):
            if g == EARLY_GROUPS[0]:
                load_planes(w)
            load_weights(w, g)
            if n < len(woven):
                load_squares(woven[n][0], woven[n][1])

        zeros = const.tile([P, N_TILE], BF16)
        nc.vector.memset(zeros[:], 0.0)
        unread = const.tile([P, 1], BF16)
        nc.scalar.copy(out=unread[:], in_=zeros[:, 0:1])
        idle_bank = psum.tile([P, N_TILE], F32, tag="bank")
        for i in range(WARM_UP):
            nc.tensor.matmul(idle_bank[:], lhsT=zeros[:, 0:P], rhs=zeros[:], start=True, stop=True)

        grouped_of = {}
        x_codes_of = {}
        x_scales_of = {}
        for g in range(G):
            plus = x_pool.tile([P, C, P, PACK], BF16, align_bytes=64)
            minus = x_pool.tile([P, C, P, PACK], BF16, align_bytes=64)
            x_codes = x_pool.tile([P, 2, C, P], U32, align_bytes=256)
            x_scales = x_pool.tile([P, 2, C, P], U8, align_bytes=256)
            grouped_of[(g, PLUS)] = plus
            grouped_of[(g, MINUS)] = minus
            x_codes_of[g] = x_codes
            x_scales_of[g] = x_scales

        def quantise(g, copy_of_x, first, count):
            nc.vector.quantize_mx(
                out=x_codes_of[g][:, copy_of_x, first : first + count, :]
                .rearrange("p c m -> p (c m)")
                .bitcast(FP8X4),
                scales=x_scales_of[g][:, copy_of_x, first : first + count, :].rearrange("p c m -> p (c m)"),
                in_=grouped_of[(g, copy_of_x)][:, first : first + count, :, :].rearrange(
                    "p c m t -> p (c m t)"
                ),
            )

        def negate(g):
            nc.vector.tensor_scalar_mul(
                out=grouped_of[(g, MINUS)][:].rearrange("p c m t -> p (c m t)"),
                in0=grouped_of[(g, PLUS)][:].rearrange("p c m t -> p (c m t)"),
                scalar1=-1.0,
            )

        for g in EARLY_GROUPS:
            for pair in range(C // 2):
                x_words = x_rows_of[(g, pair)][:].rearrange("p c k -> p (c k)").bitcast(F32)
                words_in_group = K_PASS // 2
                flipped = psum.tile([P, 2, 2, P], F32, tag="bank")
                for j in range(2):
                    for u in range(2):
                        nc.tensor.transpose(
                            flipped[:, j, u, :],
                            x_words[:, words_in_group * j + u : words_in_group * (j + 1) : 2],
                            identity[:],
                        )
                nc.scalar.copy(
                    out=grouped_of[(g, PLUS)][:, 2 * pair : 2 * pair + 2, :, :].bitcast(F32),
                    in_=flipped[:].rearrange("p j u m -> p j m u"),
                )
                quantise(g, PLUS, 2 * pair, 2)
        for g in EARLY_GROUPS:
            negate(g)
        for g in EARLY_GROUPS:
            quantise(g, MINUS, 0, C)

        def turn_late_group(g):
            words = by_square_of[g][:].rearrange("p c b e -> p (c b e)").bitcast(F32)
            sorted_words = late_pool.tile([P, C * QUADRANTS, 2, SQUARE], F32, align_bytes=64)
            nc.scalar.copy(
                out=sorted_words[:], in_=words.rearrange("p (b i u) -> p b u i", i=SQUARE, u=2)
            )
            turned = late_pool.tile([P, C * QUADRANTS * 2 * SQUARE], F32, align_bytes=64)
            nc.vector.transpose(out=turned[:], in_=sorted_words[:].rearrange("p b u i -> p (b u i)"))
            nc.scalar.copy(
                out=grouped_of[(g, PLUS)][:]
                .rearrange("p c m t -> p (c m t)")
                .bitcast(F32)
                .rearrange("p (b j u) -> p b j u", j=SQUARE, u=2),
                in_=turned[:].rearrange("p (b u j) -> p b j u", u=2, j=SQUARE),
            )
            quantise(g, PLUS, 0, C)
            negate(g)
            quantise(g, MINUS, 0, C)

        r_minus_k = const.tile([P, SQUARE], F32)
        r_plus_k = const.tile([P, SQUARE], F32)
        i_plus_j = const.tile([P, SQUARE], F32)
        i_minus_j = const.tile([P, SQUARE], F32)
        nc.vector.tensor_tensor(out=r_minus_k[:], in0=folded[:, 0, :], in1=folded[:, 3, :], op=subtract)
        nc.vector.tensor_tensor(out=r_plus_k[:], in0=folded[:, 0, :], in1=folded[:, 3, :], op=add)
        nc.vector.tensor_tensor(out=i_plus_j[:], in0=folded[:, 1, :], in1=folded[:, 2, :], op=add)
        nc.vector.tensor_tensor(out=i_minus_j[:], in0=folded[:, 1, :], in1=folded[:, 2, :], op=subtract)
        combined = const.tile([P, C, SQUARE], F32, align_bytes=64)
        nc.vector.tensor_tensor(out=combined[:, 0, :], in0=r_minus_k[:], in1=i_plus_j[:], op=subtract)
        nc.vector.tensor_tensor(out=combined[:, 1, :], in0=r_minus_k[:], in1=i_plus_j[:], op=add)
        nc.vector.tensor_tensor(out=combined[:, 2, :], in0=r_plus_k[:], in1=i_minus_j[:], op=subtract)
        nc.vector.tensor_tensor(out=combined[:, 3, :], in0=r_plus_k[:], in1=i_minus_j[:], op=add)
        upright = const.tile([P, C * SQUARE], F32, align_bytes=64)
        nc.vector.transpose(out=upright[:], in_=combined[:].rearrange("p o i -> p (o i)"))

        bias_of = []
        for s in range(2):
            repeated = bias_pool.tile([P, 2 * SQUARE, SQUARE], F32, align_bytes=64)
            nc.scalar.copy(
                out=repeated[:],
                in_=upright[:, 2 * SQUARE * s : 2 * SQUARE * (s + 1)]
                .unsqueeze(2)
                .to_broadcast([P, 2 * SQUARE, SQUARE]),
            )
            bias = bias_pool.tile([P, 2 * QO], F32, align_bytes=64)
            nc.vector.transpose(out=bias[:], in_=repeated[:].rearrange("p b j -> p (b j)"))
            bias_of.append(bias)

        for g in LATE_GROUPS:
            turn_late_group(g)

        def one_pass(acc, o, first, width, w, g, start, stop):
            c = [HAMILTON[row][o][0] for row in range(C)].index(w)
            copy_of_x = HAMILTON[c][o][1]
            nc.tensor.matmul_mx(
                out=acc[:],
                lhsT=x_codes_of[g][:, copy_of_x, c, :].bitcast(FP8X4),
                lhsT_scale=x_scales_of[g][:, copy_of_x, c, :],
                rhs=w_codes_of[(w, g)][:, first : first + width].bitcast(FP8X4),
                rhs_scale=planes_of[w][PACK * g : P, first : first + width],
                start=start,
                stop=stop,
            )

        def finish(acc, o, first, width):
            result = stage.tile([P, width], F32, tag="result")
            in_bias = QO * (o % 2) + first
            nc.vector.tensor_tensor(
                out=result[:], in0=acc[:], in1=bias_of[o // 2][:, in_bias : in_bias + width], op=add
            )
            nc.sync.dma_start(out=out[:, QO * o + first : QO * o + first + width], in_=result[:])

        swept = [(o, N_TILE * h) for h in range(H) for o in range(C)]
        acc_of = {}
        for o, first in swept:
            acc = psum.tile([P, N_TILE], F32, tag="bank")
            acc_of[(o, first)] = acc

        arrival = [(w, g) for w in range(C) for g in EARLY_GROUPS] + [
            (w, g) for g in LATE_GROUPS for w in range(C)
        ]
        for w, g in arrival[:-BANK_BY_BANK]:
            for o, first in swept:
                one_pass(acc_of[(o, first)], o, first, N_TILE, w, g, (w, g) == arrival[0], False)

        for o, first in swept:
            for w, g in arrival[-BANK_BY_BANK:]:
                one_pass(acc_of[(o, first)], o, first, N_TILE, w, g, False, (w, g) == arrival[-1])
            finish(acc_of[(o, first)], o, first, N_TILE)
